import numpy as np
import ml_dtypes


def mxq(x, axis, fmt="e4m3"):
    dtype, down = {"e4m3": (ml_dtypes.float8_e4m3fn, 7), "e5m2": (ml_dtypes.float8_e5m2, 14)}[fmt]
    v = np.moveaxis(np.asarray(x, np.float32).astype(ml_dtypes.bfloat16).astype(np.float64), axis, -1)
    blocks = v.reshape(v.shape[:-1] + (-1, 32))
    amax = np.abs(blocks).max(-1, keepdims=True)
    byte = np.maximum(np.where(amax > 0, np.frexp(amax)[1] - 1 + 127, 0) - down, 1)
    scale = np.exp2(byte - 127.0)
    codes = (blocks / scale).astype(np.float32).astype(dtype).astype(np.float64)
    return np.moveaxis((codes * scale).reshape(v.shape), -1, axis)


WIDE = False


def mx_kscale(k):
    if not WIDE:
        return np.ones(k)
    levels = np.array([18, -18])
    if k % 512:
        return np.exp2(np.random.permutation(np.resize(levels, k // 32))).repeat(32)
    a = np.empty((k // 512, 16))
    for p in range(k // 512):
        a[p, :8] = np.random.permutation(np.resize(levels, 8))
        for g in range(8):
            far = levels[np.abs(levels - a[p, g]) >= 10]
            a[p, g + 8] = far[np.random.randint(len(far))]
    return np.exp2(a.ravel()).repeat(32)


BF16 = ml_dtypes.bfloat16


def bf(x):
    return np.asarray(x, np.float32).astype(BF16)


def f64(x):
    return np.asarray(x).astype(np.float64)


B, G, WS, C, NH, LK = 1, 64, 32, 256, 4, 512
N = G * G
NW = WS * WS
NG = G // WS
BW = B * NG * NG
DH = C // NH


def setup_inputs():
    s = mx_kscale(NW)
    u = mx_kscale(LK)
    v = mx_kscale(2 * C)
    st = np.broadcast_to(s.reshape(1, 1, WS, 1, WS), (B, NG, WS, NG, WS)).reshape(B, N, 1)
    x0 = bf(np.random.standard_normal((B, N, C)))
    kv_w0 = bf(np.random.standard_normal((C, 2 * C)) / np.sqrt(C))
    kv_b = bf(np.random.standard_normal(2 * C) * 0.3)
    E_k0 = bf(np.random.standard_normal((NW, LK)) / np.sqrt(NW))
    E_v0 = bf(np.random.standard_normal((NW, LK)) * 2.0 / np.sqrt(NW))
    uj = u.reshape(1, 1, LK, 1)
    vk = v[:C].reshape(1, NH, 1, DH)
    vv = v[C:].reshape(1, NH, 1, DH)
    g0 = bf(np.random.standard_normal((BW, NH, LK, DH)) * np.exp2(np.random.randint(-6, 1, (BW, 1, LK, 1))) * uj * vk)
    g1 = bf(np.random.standard_normal((BW, NH, LK, DH)) * np.exp2(np.random.randint(-6, 1, (BW, 1, LK, 1))) * uj * vv)
    return {"x": bf(f64(x0) * st),
            "kv_w": bf(f64(kv_w0) / v),
            "kv_b": kv_b,
            "E_k": bf(f64(E_k0) / s[:, None] / u),
            "E_v": bf(f64(E_v0) / s[:, None] / u),
            "grad_0": g0,
            "grad_1": g1}


def reference(x, kv_w, kv_b, E_k, E_v, grad_0, grad_1):
    g = np.stack([f64(grad_0), f64(grad_1)])
    g = g.transpose(0, 3, 1, 2, 4).reshape(2, LK, BW * C)
    E = np.stack([f64(E_k), f64(E_v)])
    d = mxq(E, 2, "e4m3") @ mxq(g, 1, "e5m2")
    dkv = d.reshape(2, NW, BW, C).transpose(2, 1, 0, 3).reshape(BW, NW, 2 * C)
    dkv = dkv.reshape(B, NG, NG, WS, WS, 2 * C).transpose(0, 1, 3, 2, 4, 5).reshape(B * N, 2 * C)
    dx = mxq(dkv, 1, "e5m2") @ mxq(f64(kv_w), 1, "e4m3").T
    xt = f64(x).reshape(B * N, C)
    dkv_w = mxq(xt, 0, "e4m3").T @ mxq(dkv, 0, "e5m2")
    return dx.reshape(B, N, C), dkv_w

@@ -1,0 +1,465 @@
+from contextlib import ExitStack
+
+import concourse.mybir as mybir
+from concourse.masks import make_identity
+
+F32 = mybir.dt.float32
+BF16 = mybir.dt.bfloat16
+U32 = mybir.dt.uint32
+U8 = mybir.dt.uint8
+E4M3 = mybir.dt.float8_e4m3fn_x4
+E5M2 = mybir.dt.float8_e5m2_x4
+
+FLOPS = 2 * 2 * 4 * 1024 * 512 * 256 + 2 * 2 * 4096 * 512 * 256
+
+
+def tile_efficientspatialwindowattention_pa_v_kernel(
+    tc, x, kv_w, kv_b, e_k, e_v, grad_0, grad_1, out_0, out_1
+):
+    nc = tc.nc
+    es = (e_k, e_v)
+    grads = (grad_0, grad_1)
+    x_view = x.rearrange(
+        "o (a h r b q t) c -> a b h o r q (t c)", a=2, h=2, r=16, b=2, q=8, t=4
+    )
+    dx_view = out_0.rearrange(
+        "o (a h r b q t) c -> a b h o r q (t c)", a=2, h=2, r=16, b=2, q=8, t=4
+    )
+
+    with ExitStack() as ctx:
+        keep = ctx.enter_context(tc.tile_pool(name="keep", bufs=1))
+        rot = ctx.enter_context(tc.tile_pool(name="rot", bufs=3))
+        ps1 = ctx.enter_context(tc.psum_pool(name="ps1", bufs=4))
+        pst = ctx.enter_context(tc.psum_pool(name="pst", bufs=2))
+        psd = ctx.enter_context(tc.psum_pool(name="psd", bufs=2))
+
+        ident = keep.tile([128, 128], F32, name="ident")
+        e_raw = {}
+        e_in = {}
+        e_codes = {}
+        e_scales = {}
+        for kv in range(2):
+            for h in range(2):
+                e_raw[kv, h] = keep.tile([128, 4, 512], BF16, name="e_raw_%d%d" % (kv, h), align_bytes=64)
+                e_codes[kv, h] = keep.tile([128, 512], U32, name="e_codes_%d%d" % (kv, h), align_bytes=64)
+                e_scales[kv, h] = keep.tile([128, 512], U8, name="e_scales_%d%d" % (kv, h), align_bytes=64)
+        g_raw = {}
+        g_in = {}
+        g_codes = {}
+        g_scales = {}
+        for kv in range(2):
+            for w in range(4):
+                g_raw[kv, w] = keep.tile([128, 4, 4, 64], BF16, name="g_raw_%d%d" % (kv, w), align_bytes=64)
+            for wp in range(2):
+                g_codes[kv, wp] = keep.tile([128, 512], U32, name="g_codes_%d%d" % (kv, wp), align_bytes=64)
+                g_scales[kv, wp] = keep.tile([128, 512], U8, name="g_scales_%d%d" % (kv, wp), align_bytes=64)
+        x_raw = {}
+        x_in = {}
+        x_codes = {}
+        x_scales = {}
+        t_codes = {}
+        t_scales = {}
+        for n in range(4):
+            x_raw[n] = keep.tile([128, 2, 1024], BF16, name="x_raw_%d" % n, align_bytes=64)
+            x_codes[n] = keep.tile([128, 512], U32, name="x_codes_%d" % n, align_bytes=64)
+            x_scales[n] = keep.tile([128, 512], U8, name="x_scales_%d" % n, align_bytes=64)
+            for w in range(2):
+                t_codes[n, w] = keep.tile([128, 512], U32, name="t_codes_%d%d" % (n, w), align_bytes=64)
+                t_scales[n, w] = keep.tile([128, 512], U8, name="t_scales_%d%d" % (n, w), align_bytes=64)
+        kw_raw = keep.tile([128, 2, 512], BF16, name="kw_raw", align_bytes=64)
+        kw_in = keep.tile([128, 1024], BF16, name="kw_in", align_bytes=64)
+        kw_codes = keep.tile([128, 768], U32, name="kw_codes", align_bytes=64)
+        kw_scales = keep.tile([128, 768], U8, name="kw_scales", align_bytes=64)
+
+        d = {}
+        banks = {}
+        f_in = {}
+        f_codes = {}
+        f_scales = {}
+        t_in = {}
+        dx = {}
+        o1 = {}
+
+        def load_e(kv, h, tp):
+            src = es[kv].rearrange("(h p t) j -> h p t j", h=2, t=4)
+            nc.sync.dma_start(
+                out=e_raw[kv, h][:, 2 * tp : 2 * tp + 2, :], in_=src[h, :, 2 * tp : 2 * tp + 2, :]
+            )
+
+        def load_g(kv, w):
+            src = grads[kv].rearrange("w h (p j) d -> w p h (j d)", j=4)
+            nc.sync.dma_start(out=g_raw[kv, w][:].rearrange("p h j d -> p h (j d)"), in_=src[w])
+
+        def load_x(n, w):
+            nc.sync.dma_start(out=x_raw[n][:, w, :], in_=x_view[n // 2, w, n % 2, 0])
+
+        def load_kw():
+            nc.sync.dma_start(out=kw_raw[:], in_=kv_w.rearrange("(m p) k -> p m k", m=2))
+
+        def copy(eng, out, in_):
+            if eng == "V":
+                nc.vector.tensor_copy(out=out, in_=in_)
+            else:
+                nc.scalar.copy(out=out, in_=in_)
+
+        def tr_e(kv, h, tp, pool):
+            bank = pool.tile([128, 512], F32, name="bank_e", tag="b")
+            banks["e", kv, h, tp] = bank
+            for t in range(2):
+                words = e_raw[kv, h][:, 2 * tp + t, :].bitcast(F32)
+                for u in range(2):
+                    c0 = (2 * t + u) * 128
+                    nc.tensor.transpose(bank[:, c0 : c0 + 128], words[:, u::2], ident[:])
+
+        def ev_e(eng, kv, h, tp):
+            if tp == 0:
+                e_in[kv, h] = rot.tile([128, 2048], BF16, name="e_in", bufs=2, align_bytes=64)
+            bank = banks["e", kv, h, tp]
+            dst = e_in[kv, h][:].bitcast(F32)[:, tp * 512 : (tp + 1) * 512]
+            copy(
+                eng,
+                dst.rearrange("p (t r u) -> p t r u", t=2, u=2),
+                bank[:].rearrange("p (t u r) -> p t r u", t=2, u=2),
+            )
+
+        def q_e(kv, h):
+            nc.vector.quantize_mx(
+                out=e_codes[kv, h][:].bitcast(E4M3), scales=e_scales[kv, h][:], in_=e_in[kv, h][:]
+            )
+
+        def il_g(kv, w):
+            if w % 2 == 0:
+                g_in[kv, w // 2] = rot.tile([128, 2, 1024], BF16, name="g_in", bufs=2, align_bytes=64)
+            nc.vector.tensor_copy(
+                out=g_in[kv, w // 2][:, w % 2, :].rearrange("p (h d j) -> p h d j", h=4, j=4),
+                in_=g_raw[kv, w][:].rearrange("p h j d -> p h d j"),
+            )
+
+        def q_g(kv, wp):
+            nc.vector.quantize_mx(
+                out=g_codes[kv, wp][:].bitcast(E5M2),
+                scales=g_scales[kv, wp][:],
+                in_=g_in[kv, wp][:].rearrange("p w f -> p (w f)"),
+            )
+
+        def tr_kw():
+            bank = psd.tile([128, 512], F32, name="bank_kw", tag="b")
+            banks["kw"] = bank
+            for m in range(2):
+                words = kw_raw[:, m, :].bitcast(F32)
+                for u in range(2):
+                    c0 = (2 * m + u) * 128
+                    nc.tensor.transpose(bank[:, c0 : c0 + 128], words[:, u::2], ident[:])
+
+        def ev_kw(eng):
+            copy(
+                eng,
+                kw_in[:].bitcast(F32).rearrange("p (m r u) -> p m r u", m=2, u=2),
+                banks["kw"][:].rearrange("p (m u r) -> p m r u", m=2, u=2),
+            )
+
+        def q_kw():
+            nc.vector.quantize_mx(
+                out=kw_codes[:, 256:512].bitcast(E4M3), scales=kw_scales[:, 256:512], in_=kw_in[:]
+            )
+
+        def il_x(n):
+            x_in[n] = rot.tile([128, 2048], BF16, name="x_in", bufs=2, align_bytes=64)
+            nc.vector.tensor_copy(
+                out=x_in[n][:].rearrange("p (w c t) -> p w c t", w=2, t=4),
+                in_=x_raw[n][:].rearrange("p w (t c) -> p w c t", t=4),
+            )
+
+        def q_x(n):
+            nc.vector.quantize_mx(
+                out=x_codes[n][:].bitcast(E4M3), scales=x_scales[n][:], in_=x_in[n][:]
+            )
+
+        def mm_s1(n, kv, t):
+            if n not in d:
+                d[n] = rot.tile([128, 2, 4, 512], BF16, name="d", bufs=3, align_bytes=64)
+            h = n % 2
+            bank = ps1.tile([128, 512], F32, name="bank_s1", tag="b")
+            banks["s1", n, kv, t] = bank
+            cols = slice(128 * t, 128 * t + 128)
+            nc.tensor.matmul_mx(
+                out=bank[:],
+                lhsT=e_codes[kv, h][:, cols].bitcast(E4M3),
+                lhsT_scale=e_scales[kv, h][:, cols],
+                rhs=g_codes[kv, n // 2][:].bitcast(E5M2),
+                rhs_scale=g_scales[kv, n // 2][:],
+                start=True,
+                stop=True,
+            )
+
+        def ev_s1(eng, n, kv, t):
+            dst = d[n][:, :, t, :].rearrange("p w (u f) -> p w u f", u=2)[:, :, :, 128 * kv : 128 * kv + 128]
+            copy(
+                eng,
+                dst.rearrange("p w u (i e) -> p w u i e", e=2),
+                banks["s1", n, kv, t][:].rearrange("p (w i u e) -> p w u i e", w=2, u=2, e=2),
+            )
+
+        def tr_d(n, t):
+            bank = pst.tile([128, 512], F32, name="bank_t", tag="b")
+            banks["t", n, t] = bank
+            for w in range(2):
+                words = d[n][:, w, t, :].bitcast(F32)
+                for u in range(2):
+                    c0 = (2 * w + u) * 128
+                    nc.tensor.transpose(
+                        bank[:, c0 : c0 + 128], words[:, 128 * u : 128 * u + 128], ident[:]
+                    )
+
+        def ev_t(eng, n, t):
+            if t % 2 == 0:
+                f_in[n, t // 2] = rot.tile([128, 2048], BF16, name="f_in", align_bytes=64)
+            dst = f_in[n, t // 2][:].bitcast(F32)[:, (t % 2) * 512 : (t % 2) * 512 + 512]
+            copy(
+                eng,
+                dst.rearrange("p (w r u) -> p w r u", w=2, u=2),
+                banks["t", n, t][:].rearrange("p (w u r) -> p w r u", w=2, u=2),
+            )
+
+        def q_f(n, tp):
+            f_codes[n, tp] = rot.tile([128, 512], U32, name="f_codes", align_bytes=64)
+            f_scales[n, tp] = rot.tile([128, 512], U8, name="f_scales", align_bytes=64)
+            nc.vector.quantize_mx(
+                out=f_codes[n, tp][:].bitcast(E5M2), scales=f_scales[n, tp][:], in_=f_in[n, tp][:]
+            )
+
+        def mm_dx(n, tp, w):
+            bank = psd.tile([128, 512], F32, name="bank_dx", tag="b")
+            banks["dx", n, tp, w] = bank
+            for t in range(2):
+                cols = slice((2 * t + w) * 128, (2 * t + w) * 128 + 128)
+                win = slice(256, 768) if t == 0 else slice(0, 512)
+                nc.tensor.matmul_mx(
+                    out=bank[:],
+                    lhsT=f_codes[n, tp][:, cols].bitcast(E5M2),
+                    lhsT_scale=f_scales[n, tp][:, cols],
+                    rhs=kw_codes[:, win].bitcast(E4M3),
+                    rhs_scale=kw_scales[:, win],
+                    start=(t == 0),
+                    stop=(t == 1),
+                )
+
+        def ev_dx(eng, n, tp, w):
+            if tp == 0:
+                dx[n, w] = rot.tile([128, 1024], F32, name="dx", bufs=4, align_bytes=64)
+            copy(eng, dx[n, w][:, tp * 512 : tp * 512 + 512], banks["dx", n, tp, w][:])
+
+        def store_dx(n, w):
+            nc.sync.dma_start(
+                out=dx_view[n // 2, w, n % 2, 0], in_=dx[n, w][:]
+            )
+
+        def il_t(n, w):
+            t_in[n, w] = rot.tile([128, 2048], BF16, name="t_in", bufs=3, align_bytes=64)
+            nc.vector.tensor_copy(
+                out=t_in[n, w][:].rearrange("p (c t) -> p c t", t=4),
+                in_=d[n][:, w, :, :].rearrange("p t c -> p c t"),
+            )
+
+        def q_t(n, w):
+            nc.vector.quantize_mx(
+                out=t_codes[n, w][:].bitcast(E5M2), scales=t_scales[n, w][:], in_=t_in[n, w][:]
+            )
+
+        def mm_o1(n, w):
+            for m in range(2):
+                if m not in o1:
+                    bank = ps1.tile([128, 512], F32, name="bank_o1", tag="b")
+                    o1[m] = bank
+                cols = slice(256 * w + 128 * m, 256 * w + 128 * m + 128)
+                nc.tensor.matmul_mx(
+                    out=o1[m][:],
+                    lhsT=x_codes[n][:, cols].bitcast(E4M3),
+                    lhsT_scale=x_scales[n][:, cols],
+                    rhs=t_codes[n, w][:].bitcast(E5M2),
+                    rhs_scale=t_scales[n, w][:],
+                    start=(n == 0 and w == 0),
+                    stop=(n == 3 and w == 1),
+                )
+
+        def ev_o1(eng, m):
+            res = keep.tile([128, 512], F32, name="res_%d" % m, align_bytes=64)
+            copy(
+                eng,
+                res[:].rearrange("p (i u e) -> p i u e", u=2, e=2),
+                o1[m][:].rearrange("p (u i e) -> p i u e", u=2, e=2),
+            )
+            nc.sync.dma_start(out=out_1[128 * m : 128 * m + 128, :], in_=res[:])
+
+
+        with tc.manual_schedule():
+            make_identity(nc, ident[:])
+            nc.gpsimd.memset(kw_codes[:, 0:256], 0)
+            nc.gpsimd.memset(kw_codes[:, 512:768], 0)
+            nc.gpsimd.memset(kw_scales[:].bitcast(U32)[:, 0:64], 0)
+            nc.gpsimd.memset(kw_scales[:].bitcast(U32)[:, 128:192], 0)
+            load_e(0, 0, 0)
+            load_g(0, 0)
+            load_g(0, 1)
+            load_e(0, 0, 1)
+            load_e(1, 0, 0)
+            load_e(1, 0, 1)
+            load_g(1, 0)
+            load_g(1, 1)
+            load_x(0, 0)
+            load_x(0, 1)
+            load_e(0, 1, 0)
+            load_e(0, 1, 1)
+            load_g(0, 2)
+            load_g(0, 3)
+            load_e(1, 1, 0)
+            load_e(1, 1, 1)
+            load_kw()
+            load_g(1, 2)
+            load_g(1, 3)
+            for n in range(1, 4):
+                for w in range(2):
+                    load_x(n, w)
+
+            tr_e(0, 0, 0, pst)
+            ev_e("S", 0, 0, 0)
+            il_g(0, 0)
+            il_g(0, 1)
+            tr_e(0, 0, 1, pst)
+            ev_e("S", 0, 0, 1)
+            tr_e(1, 0, 0, psd)
+            tr_e(1, 0, 1, psd)
+            ev_e("S", 1, 0, 0)
+            ev_e("S", 1, 0, 1)
+            q_g(0, 0)
+            q_e(0, 0)
+            for t in range(4):
+                mm_s1(0, 0, t)
+                ev_s1("S", 0, 0, t)
+            il_g(1, 0)
+            il_g(1, 1)
+            q_e(1, 0)
+            q_g(1, 0)
+            il_x(0)
+            for t in range(4):
+                mm_s1(0, 1, t)
+            tr_e(0, 1, 0, psd)
+            tr_e(0, 1, 1, psd)
+            for t in range(4):
+                ev_s1("S", 0, 1, t)
+            il_g(0, 2)
+            q_x(0)
+            il_g(0, 3)
+            ev_e("S", 0, 1, 0)
+            ev_e("S", 0, 1, 1)
+            for t in (0, 1):
+                tr_d(0, t)
+            tr_e(1, 1, 0, psd)
+            tr_e(1, 1, 1, psd)
+            ev_t("S", 0, 0)
+            ev_t("S", 0, 1)
+            il_t(0, 0)
+            q_e(0, 1)
+            q_g(0, 1)
+            for t in range(4):
+                mm_s1(1, 0, t)
+            for t in (2, 3):
+                tr_d(0, t)
+            for t in range(4):
+                ev_s1("S", 1, 0, t)
+            ev_e("S", 1, 1, 0)
+            ev_e("S", 1, 1, 1)
+            il_t(0, 1)
+            q_f(0, 0)
+            q_t(0, 0)
+            q_e(1, 1)
+            tr_kw()
+            ev_kw("S")
+            il_g(1, 2)
+            il_g(1, 3)
+            q_t(0, 1)
+            q_kw()
+            q_g(1, 1)
+            for t in range(4):
+                mm_s1(1, 1, t)
+            ev_t("S", 0, 2)
+            ev_t("S", 0, 3)
+            q_f(0, 1)
+            mm_dx(0, 0, 0)
+            mm_dx(0, 0, 1)
+            for t in range(4):
+                ev_s1("S", 1, 1, t)
+            ev_dx("S", 0, 0, 0)
+            ev_dx("S", 0, 0, 1)
+            il_x(1)
+            for i in range(4, 8):
+                n, tp = divmod(i, 2)
+                m, mp = divmod(i - 1, 2)
+                l, lp = divmod(i - 2, 2)
+                s1 = [(n, kv, t) for t in (2 * tp, 2 * tp + 1) for kv in range(2)]
+                if i == 4:
+                    for t in (0, 1):
+                        tr_d(1, t)
+                    mm_dx(0, 1, 0)
+                    mm_dx(0, 1, 1)
+                    ev_t("S", 1, 0)
+                    ev_t("S", 1, 1)
+                    il_t(1, 0)
+                    q_x(1)
+                    q_f(1, 0)
+                for a in s1:
+                    mm_s1(*a)
+                if i == 4:
+                    ev_dx("S", 0, 1, 0)
+                    ev_dx("S", 0, 1, 1)
+                    store_dx(0, 0)
+                    store_dx(0, 1)
+                for a in s1:
+                    ev_s1("S", *a)
+                for t in (2 * mp, 2 * mp + 1):
+                    tr_d(m, t)
+                    ev_t("S", m, t)
+                mm_dx(l, lp, 0)
+                mm_dx(l, lp, 1)
+                ev_dx("S", l, lp, 0)
+                if mp == 1 and m < 3:
+                    if m > 1:
+                        il_t(m, 0)
+                    il_t(m, 1)
+                    q_t(m, 0)
+                q_f(m, mp)
+                if mp == 1 and m < 3:
+                    q_t(m, 1)
+                ev_dx("S", l, lp, 1)
+                if i in (4, 5):
+                    il_x(i - 2)
+                if i in (5, 6):
+                    q_x(i - 3)
+                if lp == 1:
+                    store_dx(l, 0)
+                    store_dx(l, 1)
+            il_t(3, 0)
+            for t in (2, 3):
+                tr_d(3, t)
+                ev_t("S", 3, t)
+            mm_dx(3, 0, 0)
+            mm_dx(3, 0, 1)
+            ev_dx("S", 3, 0, 0)
+            ev_dx("S", 3, 0, 1)
+            q_f(3, 1)
+            il_t(3, 1)
+            q_t(3, 0)
+            q_t(3, 1)
+            for k in range(3):
+                mm_o1(k, 0)
+                mm_o1(k, 1)
+            mm_dx(3, 1, 0)
+            mm_dx(3, 1, 1)
+            ev_dx("S", 3, 1, 0)
+            ev_dx("S", 3, 1, 1)
+            store_dx(3, 0)
+            store_dx(3, 1)
+            mm_o1(3, 0)
+            mm_o1(3, 1)
+            ev_o1("S", 0)
+            ev_o1("V", 1)

@@ -222,8 +222,8 @@ def tile_efficientspatialwindowattention_pa_v_kernel(
             )
 
         def q_f(n, tp):
-            f_codes[n, tp] = rot.tile([128, 512], U32, name="f_codes", align_bytes=64)
-            f_scales[n, tp] = rot.tile([128, 512], U8, name="f_scales", align_bytes=64)
+            f_codes[n, tp] = rot.tile([128, 512], U32, name="f_codes", bufs=4, align_bytes=64)
+            f_scales[n, tp] = rot.tile([128, 512], U8, name="f_scales", bufs=4, align_bytes=64)
             nc.vector.quantize_mx(
                 out=f_codes[n, tp][:].bitcast(E5M2), scales=f_scales[n, tp][:], in_=f_in[n, tp][:]
             )
@@ -249,9 +249,10 @@ def tile_efficientspatialwindowattention_pa_v_kernel(
                 dx[n, w] = rot.tile([128, 1024], F32, name="dx", bufs=4, align_bytes=64)
             copy(eng, dx[n, w][:, tp * 512 : tp * 512 + 512], banks["dx", n, tp, w][:])
 
-        def store_dx(n, w):
+        def store_dx(n, w, tp=None):
+            rows = slice(0, 1024) if tp is None else slice(512 * tp, 512 * tp + 512)
             nc.sync.dma_start(
-                out=dx_view[n // 2, w, n % 2, 0], in_=dx[n, w][:]
+                out=dx_view[n // 2, w, n % 2, 0][:, :, rows], in_=dx[n, w][:, rows]
             )
 
         def il_t(n, w):
@@ -345,120 +346,78 @@ def tile_efficientspatialwindowattention_pa_v_kernel(
                 mm_s1(0, 1, t)
             tr_e(0, 1, 0, psd)
             tr_e(0, 1, 1, psd)
-            for t in range(4):
-                ev_s1("S", 0, 1, t)
-            il_g(0, 2)
-            q_x(0)
-            il_g(0, 3)
+            ev_s1("S", 0, 1, 0)
+            ev_s1("S", 0, 1, 1)
             ev_e("S", 0, 1, 0)
             ev_e("S", 0, 1, 1)
-            for t in (0, 1):
-                tr_d(0, t)
+            tr_d(0, 0)
+            tr_d(0, 1)
             tr_e(1, 1, 0, psd)
             tr_e(1, 1, 1, psd)
+            ev_s1("S", 0, 1, 2)
+            ev_s1("S", 0, 1, 3)
+            ev_e("S", 1, 1, 0)
+            ev_e("S", 1, 1, 1)
+            il_g(0, 2)
+            q_x(0)
+            q_e(0, 1)
+            il_g(0, 3)
             ev_t("S", 0, 0)
             ev_t("S", 0, 1)
             il_t(0, 0)
-            q_e(0, 1)
-            q_g(0, 1)
-            for t in range(4):
-                mm_s1(1, 0, t)
-            for t in (2, 3):
-                tr_d(0, t)
-            for t in range(4):
-                ev_s1("S", 1, 0, t)
-            ev_e("S", 1, 1, 0)
-            ev_e("S", 1, 1, 1)
-            il_t(0, 1)
-            q_f(0, 0)
-            q_t(0, 0)
             q_e(1, 1)
+            q_g(0, 1)
             tr_kw()
-            ev_kw("S")
-            il_g(1, 2)
-            il_g(1, 3)
-            q_t(0, 1)
+            ev_kw("V")
+            q_f(0, 0)
             q_kw()
-            q_g(1, 1)
-            for t in range(4):
-                mm_s1(1, 1, t)
-            ev_t("S", 0, 2)
-            ev_t("S", 0, 3)
-            q_f(0, 1)
-            mm_dx(0, 0, 0)
-            mm_dx(0, 0, 1)
-            for t in range(4):
-                ev_s1("S", 1, 1, t)
-            ev_dx("S", 0, 0, 0)
-            ev_dx("S", 0, 0, 1)
-            il_x(1)
-            for i in range(4, 8):
+            for i in range(2, 11):
                 n, tp = divmod(i, 2)
                 m, mp = divmod(i - 1, 2)
-                l, lp = divmod(i - 2, 2)
-                s1 = [(n, kv, t) for t in (2 * tp, 2 * tp + 1) for kv in range(2)]
-                if i == 4:
-                    for t in (0, 1):
-                        tr_d(1, t)
-                    mm_dx(0, 1, 0)
-                    mm_dx(0, 1, 1)
-                    ev_t("S", 1, 0)
-                    ev_t("S", 1, 1)
-                    il_t(1, 0)
-                    q_x(1)
-                    q_f(1, 0)
+                l, lp = divmod(i - 3, 2)
+                if i < 8:
+                    s1 = [(n, kv, t) for t in (2 * tp, 2 * tp + 1) for kv in range(2)]
+                else:
+                    s1 = []
                 for a in s1:
                     mm_s1(*a)
-                if i == 4:
-                    ev_dx("S", 0, 1, 0)
-                    ev_dx("S", 0, 1, 1)
-                    store_dx(0, 0)
-                    store_dx(0, 1)
+                if i > 7:
+                    mm_o1(i - 8, 0)
+                    mm_o1(i - 8, 1)
                 for a in s1:
                     ev_s1("S", *a)
-                for t in (2 * mp, 2 * mp + 1):
-                    tr_d(m, t)
-                    ev_t("S", m, t)
-                mm_dx(l, lp, 0)
-                mm_dx(l, lp, 1)
-                ev_dx("S", l, lp, 0)
-                if mp == 1 and m < 3:
-                    if m > 1:
-                        il_t(m, 0)
-                    il_t(m, 1)
-                    q_t(m, 0)
-                q_f(m, mp)
-                if mp == 1 and m < 3:
-                    q_t(m, 1)
-                ev_dx("S", l, lp, 1)
-                if i in (4, 5):
-                    il_x(i - 2)
-                if i in (5, 6):
-                    q_x(i - 3)
-                if lp == 1:
-                    store_dx(l, 0)
-                    store_dx(l, 1)
-            il_t(3, 0)
-            for t in (2, 3):
-                tr_d(3, t)
-                ev_t("S", 3, t)
-            mm_dx(3, 0, 0)
-            mm_dx(3, 0, 1)
-            ev_dx("S", 3, 0, 0)
-            ev_dx("S", 3, 0, 1)
-            q_f(3, 1)
-            il_t(3, 1)
-            q_t(3, 0)
-            q_t(3, 1)
-            for k in range(3):
-                mm_o1(k, 0)
-                mm_o1(k, 1)
-            mm_dx(3, 1, 0)
-            mm_dx(3, 1, 1)
-            ev_dx("S", 3, 1, 0)
-            ev_dx("S", 3, 1, 1)
-            store_dx(3, 0)
-            store_dx(3, 1)
+                if i < 9:
+                    for t in (2 * mp, 2 * mp + 1):
+                        tr_d(m, t)
+                        ev_t("S", m, t)
+                if i > 2:
+                    mm_dx(l, lp, 0)
+                    mm_dx(l, lp, 1)
+                    ev_dx("S", l, lp, 0)
+                    ev_dx("V" if i in (4, 5) else "S", l, lp, 1)
+                    if l == 3:
+                        store_dx(l, 0, lp)
+                        store_dx(l, 1, lp)
+                    elif lp == 1:
+                        store_dx(l, 0)
+                        store_dx(l, 1)
+                if 2 < i < 10:
+                    il_t((i - 2) // 2, i % 2)
+                if i == 2:
+                    il_g(1, 2)
+                    il_g(1, 3)
+                if i < 9:
+                    q_f(m, mp)
+                if 3 < i < 11:
+                    q_t((i - 3) // 2, (i - 3) % 2)
+                if i == 2:
+                    q_g(1, 1)
+                if i == 3:
+                    q_t(0, 0)
+                if i in [2,3,5]:
+                    il_x([2,3,5].index(i) + 1)
+                if i in [3,4,6]:
+                    q_x([3,4,6].index(i) + 1)
             mm_o1(3, 0)
             mm_o1(3, 1)
             ev_o1("S", 0)

@@ -131,8 +131,8 @@ def tile_efficientspatialwindowattention_pa_v_kernel(
             if w % 2 == 0:
                 g_in[kv, w // 2] = rot.tile([128, 2, 1024], BF16, name="g_in", bufs=2, align_bytes=64)
             nc.vector.tensor_copy(
-                out=g_in[kv, w // 2][:, w % 2, :].rearrange("p (h d j) -> p h d j", h=4, j=4),
-                in_=g_raw[kv, w][:].rearrange("p h j d -> p h d j"),
+                out=g_in[kv, w // 2][:, w % 2, :].rearrange("p (h d i j) -> p h d j i", h=4, i=4, j=4),
+                in_=g_raw[kv, w][:].rearrange("p h j (d i) -> p h d j i", i=4),
             )
 
         def q_g(kv, wp):
@@ -166,8 +166,8 @@ def tile_efficientspatialwindowattention_pa_v_kernel(
         def il_x(n):
             x_in[n] = rot.tile([128, 2048], BF16, name="x_in", bufs=2, align_bytes=64)
             nc.vector.tensor_copy(
-                out=x_in[n][:].rearrange("p (w c t) -> p w c t", w=2, t=4),
-                in_=x_raw[n][:].rearrange("p w (t c) -> p w c t", t=4),
+                out=x_in[n][:].rearrange("p (w c i t) -> p w c t i", w=2, i=4, t=4),
+                in_=x_raw[n][:].rearrange("p w (t c i) -> p w c t i", i=4, t=4),
             )
 
         def q_x(n):
@@ -212,7 +212,7 @@ def tile_efficientspatialwindowattention_pa_v_kernel(
                     )
 
         def ev_t(eng, n, t):
-            if t % 2 == 0:
+            if (n, t // 2) not in f_in:
                 f_in[n, t // 2] = rot.tile([128, 2048], BF16, name="f_in", align_bytes=64)
             dst = f_in[n, t // 2][:].bitcast(F32)[:, (t % 2) * 512 : (t % 2) * 512 + 512]
             copy(
@@ -245,7 +245,7 @@ def tile_efficientspatialwindowattention_pa_v_kernel(
                 )
 
         def ev_dx(eng, n, tp, w):
-            if tp == 0:
+            if (n, w) not in dx:
                 dx[n, w] = rot.tile([128, 1024], F32, name="dx", bufs=4, align_bytes=64)
             copy(eng, dx[n, w][:, tp * 512 : tp * 512 + 512], banks["dx", n, tp, w][:])
 
@@ -258,8 +258,8 @@ def tile_efficientspatialwindowattention_pa_v_kernel(
         def il_t(n, w):
             t_in[n, w] = rot.tile([128, 2048], BF16, name="t_in", bufs=3, align_bytes=64)
             nc.vector.tensor_copy(
-                out=t_in[n, w][:].rearrange("p (c t) -> p c t", t=4),
-                in_=d[n][:, w, :, :].rearrange("p t c -> p c t"),
+                out=t_in[n, w][:].rearrange("p (c i t) -> p c t i", i=4, t=4),
+                in_=d[n][:, w, :, :].rearrange("p t (c i) -> p c t i", i=4),
             )
 
         def q_t(n, w):

@@ -360,8 +360,8 @@ def tile_efficientspatialwindowattention_pa_v_kernel(
             ev_e("S", 1, 1, 1)
             il_g(0, 2)
             q_x(0)
-            q_e(0, 1)
             il_g(0, 3)
+            q_e(0, 1)
             ev_t("S", 0, 0)
             ev_t("S", 0, 1)
             il_t(0, 0)
@@ -384,23 +384,20 @@ def tile_efficientspatialwindowattention_pa_v_kernel(
                 if i > 7:
                     mm_o1(i - 8, 0)
                     mm_o1(i - 8, 1)
-                for a in s1:
+                for a in (s1[3:] + s1[:3] if i > 3 else s1):
                     ev_s1("S", *a)
                 if i < 9:
-                    for t in (2 * mp, 2 * mp + 1):
-                        tr_d(m, t)
-                        ev_t("S", m, t)
+                    tr_d(m, 2 * mp)
+                    tr_d(m, 2 * mp + 1)
+                    ev_t("S", m, 2 * mp + 1)
+                    ev_t("S", m, 2 * mp)
                 if i > 2:
                     mm_dx(l, lp, 0)
                     mm_dx(l, lp, 1)
                     ev_dx("S", l, lp, 0)
-                    ev_dx("V" if i in (4, 5) else "S", l, lp, 1)
-                    if l == 3:
-                        store_dx(l, 0, lp)
-                        store_dx(l, 1, lp)
-                    elif lp == 1:
-                        store_dx(l, 0)
-                        store_dx(l, 1)
+                    ev_dx("V" if i in (4, 5, 6) else "S", l, lp, 1)
+                    store_dx(l, 0, lp)
+                    store_dx(l, 1, lp)
                 if 2 < i < 10:
                     il_t((i - 2) // 2, i % 2)
                 if i == 2:

from contextlib import ExitStack

import concourse.mybir as mybir
from concourse.masks import make_identity

F32 = mybir.dt.float32
BF16 = mybir.dt.bfloat16
U32 = mybir.dt.uint32
U8 = mybir.dt.uint8
E4M3 = mybir.dt.float8_e4m3fn_x4
E5M2 = mybir.dt.float8_e5m2_x4

FLOPS = 2 * 2 * 4 * 1024 * 512 * 256 + 2 * 2 * 4096 * 512 * 256


def tile_efficientspatialwindowattention_pa_v_kernel(
    tc, x, kv_w, kv_b, e_k, e_v, grad_0, grad_1, out_0, out_1
):
    nc = tc.nc
    es = (e_k, e_v)
    grads = (grad_0, grad_1)
    x_view = x.rearrange(
        "o (a h r b q t) c -> a b h o r q (t c)", a=2, h=2, r=16, b=2, q=8, t=4
    )
    dx_view = out_0.rearrange(
        "o (a h r b q t) c -> a b h o r q (t c)", a=2, h=2, r=16, b=2, q=8, t=4
    )

    with ExitStack() as ctx:
        keep = ctx.enter_context(tc.tile_pool(name="keep", bufs=1))
        rot = ctx.enter_context(tc.tile_pool(name="rot", bufs=3))
        ps1 = ctx.enter_context(tc.psum_pool(name="ps1", bufs=4))
        pst = ctx.enter_context(tc.psum_pool(name="pst", bufs=2))
        psd = ctx.enter_context(tc.psum_pool(name="psd", bufs=2))

        ident = keep.tile([128, 128], F32, name="ident")
        e_raw = {}
        e_in = {}
        e_codes = {}
        e_scales = {}
        for kv in range(2):
            for h in range(2):
                e_raw[kv, h] = keep.tile([128, 4, 512], BF16, name="e_raw_%d%d" % (kv, h), align_bytes=64)
                e_codes[kv, h] = keep.tile([128, 512], U32, name="e_codes_%d%d" % (kv, h), align_bytes=64)
                e_scales[kv, h] = keep.tile([128, 512], U8, name="e_scales_%d%d" % (kv, h), align_bytes=64)
        g_raw = {}
        g_in = {}
        g_codes = {}
        g_scales = {}
        for kv in range(2):
            for w in range(4):
                g_raw[kv, w] = keep.tile([128, 4, 4, 64], BF16, name="g_raw_%d%d" % (kv, w), align_bytes=64)
            for wp in range(2):
                g_codes[kv, wp] = keep.tile([128, 512], U32, name="g_codes_%d%d" % (kv, wp), align_bytes=64)
                g_scales[kv, wp] = keep.tile([128, 512], U8, name="g_scales_%d%d" % (kv, wp), align_bytes=64)
        x_raw = {}
        x_in = {}
        x_codes = {}
        x_scales = {}
        t_codes = {}
        t_scales = {}
        for n in range(4):
            x_raw[n] = keep.tile([128, 2, 1024], BF16, name="x_raw_%d" % n, align_bytes=64)
            x_codes[n] = keep.tile([128, 512], U32, name="x_codes_%d" % n, align_bytes=64)
            x_scales[n] = keep.tile([128, 512], U8, name="x_scales_%d" % n, align_bytes=64)
            for w in range(2):
                t_codes[n, w] = keep.tile([128, 512], U32, name="t_codes_%d%d" % (n, w), align_bytes=64)
                t_scales[n, w] = keep.tile([128, 512], U8, name="t_scales_%d%d" % (n, w), align_bytes=64)
        kw_raw = keep.tile([128, 2, 512], BF16, name="kw_raw", align_bytes=64)
        kw_in = keep.tile([128, 1024], BF16, name="kw_in", align_bytes=64)
        kw_codes = keep.tile([128, 768], U32, name="kw_codes", align_bytes=64)
        kw_scales = keep.tile([128, 768], U8, name="kw_scales", align_bytes=64)

        d = {}
        banks = {}
        f_in = {}
        f_codes = {}
        f_scales = {}
        t_in = {}
        dx = {}
        o1 = {}

        def load_e(kv, h, tp):
            src = es[kv].rearrange("(h p t) j -> h p t j", h=2, t=4)
            nc.sync.dma_start(
                out=e_raw[kv, h][:, 2 * tp : 2 * tp + 2, :], in_=src[h, :, 2 * tp : 2 * tp + 2, :]
            )

        def load_g(kv, w):
            src = grads[kv].rearrange("w h (p j) d -> w p h (j d)", j=4)
            nc.sync.dma_start(out=g_raw[kv, w][:].rearrange("p h j d -> p h (j d)"), in_=src[w])

        def load_x(n, w):
            nc.sync.dma_start(out=x_raw[n][:, w, :], in_=x_view[n // 2, w, n % 2, 0])

        def load_kw():
            nc.sync.dma_start(out=kw_raw[:], in_=kv_w.rearrange("(m p) k -> p m k", m=2))

        def copy(eng, out, in_):
            if eng == "V":
                nc.vector.tensor_copy(out=out, in_=in_)
            else:
                nc.scalar.copy(out=out, in_=in_)

        def tr_e(kv, h, tp, pool):
            bank = pool.tile([128, 512], F32, name="bank_e", tag="b")
            banks["e", kv, h, tp] = bank
            for t in range(2):
                words = e_raw[kv, h][:, 2 * tp + t, :].bitcast(F32)
                for u in range(2):
                    c0 = (2 * t + u) * 128
                    nc.tensor.transpose(bank[:, c0 : c0 + 128], words[:, u::2], ident[:])

        def ev_e(eng, kv, h, tp):
            if tp == 0:
                e_in[kv, h] = rot.tile([128, 2048], BF16, name="e_in", bufs=2, align_bytes=64)
            bank = banks["e", kv, h, tp]
            dst = e_in[kv, h][:].bitcast(F32)[:, tp * 512 : (tp + 1) * 512]
            copy(
                eng,
                dst.rearrange("p (t r u) -> p t r u", t=2, u=2),
                bank[:].rearrange("p (t u r) -> p t r u", t=2, u=2),
            )

        def q_e(kv, h):
            nc.vector.quantize_mx(
                out=e_codes[kv, h][:].bitcast(E4M3), scales=e_scales[kv, h][:], in_=e_in[kv, h][:]
            )

        def il_g(kv, w):
            if w % 2 == 0:
                g_in[kv, w // 2] = rot.tile([128, 2, 1024], BF16, name="g_in", bufs=2, align_bytes=64)
            nc.vector.tensor_copy(
                out=g_in[kv, w // 2][:, w % 2, :].rearrange("p (h d i j) -> p h d j i", h=4, i=4, j=4),
                in_=g_raw[kv, w][:].rearrange("p h j (d i) -> p h d j i", i=4),
            )

        def q_g(kv, wp):
            nc.vector.quantize_mx(
                out=g_codes[kv, wp][:].bitcast(E5M2),
                scales=g_scales[kv, wp][:],
                in_=g_in[kv, wp][:].rearrange("p w f -> p (w f)"),
            )

        def tr_kw():
            bank = psd.tile([128, 512], F32, name="bank_kw", tag="b")
            banks["kw"] = bank
            for m in range(2):
                words = kw_raw[:, m, :].bitcast(F32)
                for u in range(2):
                    c0 = (2 * m + u) * 128
                    nc.tensor.transpose(bank[:, c0 : c0 + 128], words[:, u::2], ident[:])

        def ev_kw(eng):
            copy(
                eng,
                kw_in[:].bitcast(F32).rearrange("p (m r u) -> p m r u", m=2, u=2),
                banks["kw"][:].rearrange("p (m u r) -> p m r u", m=2, u=2),
            )

        def q_kw():
            nc.vector.quantize_mx(
                out=kw_codes[:, 256:512].bitcast(E4M3), scales=kw_scales[:, 256:512], in_=kw_in[:]
            )

        def il_x(n):
            x_in[n] = rot.tile([128, 2048], BF16, name="x_in", bufs=2, align_bytes=64)
            nc.vector.tensor_copy(
                out=x_in[n][:].rearrange("p (w c i t) -> p w c t i", w=2, i=4, t=4),
                in_=x_raw[n][:].rearrange("p w (t c i) -> p w c t i", i=4, t=4),
            )

        def q_x(n):
            nc.vector.quantize_mx(
                out=x_codes[n][:].bitcast(E4M3), scales=x_scales[n][:], in_=x_in[n][:]
            )

        def mm_s1(n, kv, t):
            if n not in d:
                d[n] = rot.tile([128, 2, 4, 512], BF16, name="d", bufs=3, align_bytes=64)
            h = n % 2
            bank = ps1.tile([128, 512], F32, name="bank_s1", tag="b")
            banks["s1", n, kv, t] = bank
            cols = slice(128 * t, 128 * t + 128)
            nc.tensor.matmul_mx(
                out=bank[:],
                lhsT=e_codes[kv, h][:, cols].bitcast(E4M3),
                lhsT_scale=e_scales[kv, h][:, cols],
                rhs=g_codes[kv, n // 2][:].bitcast(E5M2),
                rhs_scale=g_scales[kv, n // 2][:],
                start=True,
                stop=True,
            )

        def ev_s1(eng, n, kv, t):
            dst = d[n][:, :, t, :].rearrange("p w (u f) -> p w u f", u=2)[:, :, :, 128 * kv : 128 * kv + 128]
            copy(
                eng,
                dst.rearrange("p w u (i e) -> p w u i e", e=2),
                banks["s1", n, kv, t][:].rearrange("p (w i u e) -> p w u i e", w=2, u=2, e=2),
            )

        def tr_d(n, t):
            bank = pst.tile([128, 512], F32, name="bank_t", tag="b")
            banks["t", n, t] = bank
            for w in range(2):
                words = d[n][:, w, t, :].bitcast(F32)
                for u in range(2):
                    c0 = (2 * w + u) * 128
                    nc.tensor.transpose(
                        bank[:, c0 : c0 + 128], words[:, 128 * u : 128 * u + 128], ident[:]
                    )

        def ev_t(eng, n, t):
            if (n, t // 2) not in f_in:
                f_in[n, t // 2] = rot.tile([128, 2048], BF16, name="f_in", align_bytes=64)
            dst = f_in[n, t // 2][:].bitcast(F32)[:, (t % 2) * 512 : (t % 2) * 512 + 512]
            copy(
                eng,
                dst.rearrange("p (w r u) -> p w r u", w=2, u=2),
                banks["t", n, t][:].rearrange("p (w u r) -> p w r u", w=2, u=2),
            )

        def q_f(n, tp):
            f_codes[n, tp] = rot.tile([128, 512], U32, name="f_codes", bufs=4, align_bytes=64)
            f_scales[n, tp] = rot.tile([128, 512], U8, name="f_scales", bufs=4, align_bytes=64)
            nc.vector.quantize_mx(
                out=f_codes[n, tp][:].bitcast(E5M2), scales=f_scales[n, tp][:], in_=f_in[n, tp][:]
            )

        def mm_dx(n, tp, w):
            bank = psd.tile([128, 512], F32, name="bank_dx", tag="b")
            banks["dx", n, tp, w] = bank
            for t in range(2):
                cols = slice((2 * t + w) * 128, (2 * t + w) * 128 + 128)
                win = slice(256, 768) if t == 0 else slice(0, 512)
                nc.tensor.matmul_mx(
                    out=bank[:],
                    lhsT=f_codes[n, tp][:, cols].bitcast(E5M2),
                    lhsT_scale=f_scales[n, tp][:, cols],
                    rhs=kw_codes[:, win].bitcast(E4M3),
                    rhs_scale=kw_scales[:, win],
                    start=(t == 0),
                    stop=(t == 1),
                )

        def ev_dx(eng, n, tp, w):
            if (n, w) not in dx:
                dx[n, w] = rot.tile([128, 1024], F32, name="dx", bufs=4, align_bytes=64)
            copy(eng, dx[n, w][:, tp * 512 : tp * 512 + 512], banks["dx", n, tp, w][:])

        def store_dx(n, w, tp=None):
            rows = slice(0, 1024) if tp is None else slice(512 * tp, 512 * tp + 512)
            nc.sync.dma_start(
                out=dx_view[n // 2, w, n % 2, 0][:, :, rows], in_=dx[n, w][:, rows]
            )

        def il_t(n, w):
            t_in[n, w] = rot.tile([128, 2048], BF16, name="t_in", bufs=3, align_bytes=64)
            nc.vector.tensor_copy(
                out=t_in[n, w][:].rearrange("p (c i t) -> p c t i", i=4, t=4),
                in_=d[n][:, w, :, :].rearrange("p t (c i) -> p c t i", i=4),
            )

        def q_t(n, w):
            nc.vector.quantize_mx(
                out=t_codes[n, w][:].bitcast(E5M2), scales=t_scales[n, w][:], in_=t_in[n, w][:]
            )

        def mm_o1(n, w):
            for m in range(2):
                if m not in o1:
                    bank = ps1.tile([128, 512], F32, name="bank_o1", tag="b")
                    o1[m] = bank
                cols = slice(256 * w + 128 * m, 256 * w + 128 * m + 128)
                nc.tensor.matmul_mx(
                    out=o1[m][:],
                    lhsT=x_codes[n][:, cols].bitcast(E4M3),
                    lhsT_scale=x_scales[n][:, cols],
                    rhs=t_codes[n, w][:].bitcast(E5M2),
                    rhs_scale=t_scales[n, w][:],
                    start=(n == 0 and w == 0),
                    stop=(n == 3 and w == 1),
                )

        def ev_o1(eng, m):
            res = keep.tile([128, 512], F32, name="res_%d" % m, align_bytes=64)
            copy(
                eng,
                res[:].rearrange("p (i u e) -> p i u e", u=2, e=2),
                o1[m][:].rearrange("p (u i e) -> p i u e", u=2, e=2),
            )
            nc.sync.dma_start(out=out_1[128 * m : 128 * m + 128, :], in_=res[:])


        with tc.manual_schedule():
            make_identity(nc, ident[:])
            nc.gpsimd.memset(kw_codes[:, 0:256], 0)
            nc.gpsimd.memset(kw_codes[:, 512:768], 0)
            nc.gpsimd.memset(kw_scales[:].bitcast(U32)[:, 0:64], 0)
            nc.gpsimd.memset(kw_scales[:].bitcast(U32)[:, 128:192], 0)
            load_e(0, 0, 0)
            load_g(0, 0)
            load_g(0, 1)
            load_e(0, 0, 1)
            load_e(1, 0, 0)
            load_e(1, 0, 1)
            load_g(1, 0)
            load_g(1, 1)
            load_x(0, 0)
            load_x(0, 1)
            load_e(0, 1, 0)
            load_e(0, 1, 1)
            load_g(0, 2)
            load_g(0, 3)
            load_e(1, 1, 0)
            load_e(1, 1, 1)
            load_kw()
            load_g(1, 2)
            load_g(1, 3)
            for n in range(1, 4):
                for w in range(2):
                    load_x(n, w)

            tr_e(0, 0, 0, pst)
            ev_e("S", 0, 0, 0)
            il_g(0, 0)
            il_g(0, 1)
            tr_e(0, 0, 1, pst)
            ev_e("S", 0, 0, 1)
            tr_e(1, 0, 0, psd)
            tr_e(1, 0, 1, psd)
            ev_e("S", 1, 0, 0)
            ev_e("S", 1, 0, 1)
            q_g(0, 0)
            q_e(0, 0)
            for t in range(4):
                mm_s1(0, 0, t)
                ev_s1("S", 0, 0, t)
            il_g(1, 0)
            il_g(1, 1)
            q_e(1, 0)
            q_g(1, 0)
            il_x(0)
            for t in range(4):
                mm_s1(0, 1, t)
            tr_e(0, 1, 0, psd)
            tr_e(0, 1, 1, psd)
            ev_s1("S", 0, 1, 0)
            ev_s1("S", 0, 1, 1)
            ev_e("S", 0, 1, 0)
            ev_e("S", 0, 1, 1)
            tr_d(0, 0)
            tr_d(0, 1)
            tr_e(1, 1, 0, psd)
            tr_e(1, 1, 1, psd)
            ev_s1("S", 0, 1, 2)
            ev_s1("S", 0, 1, 3)
            ev_e("S", 1, 1, 0)
            ev_e("S", 1, 1, 1)
            il_g(0, 2)
            q_x(0)
            il_g(0, 3)
            q_e(0, 1)
            ev_t("S", 0, 0)
            ev_t("S", 0, 1)
            il_t(0, 0)
            q_e(1, 1)
            q_g(0, 1)
            tr_kw()
            ev_kw("V")
            q_f(0, 0)
            q_kw()
            for i in range(2, 11):
                n, tp = divmod(i, 2)
                m, mp = divmod(i - 1, 2)
                l, lp = divmod(i - 3, 2)
                if i < 8:
                    s1 = [(n, kv, t) for t in (2 * tp, 2 * tp + 1) for kv in range(2)]
                else:
                    s1 = []
                for a in s1:
                    mm_s1(*a)
                if i > 7:
                    mm_o1(i - 8, 0)
                    mm_o1(i - 8, 1)
                for a in (s1[3:] + s1[:3] if i > 3 else s1):
                    ev_s1("S", *a)
                if i < 9:
                    tr_d(m, 2 * mp)
                    tr_d(m, 2 * mp + 1)
                    ev_t("S", m, 2 * mp + 1)
                    ev_t("S", m, 2 * mp)
                if i > 2:
                    mm_dx(l, lp, 0)
                    mm_dx(l, lp, 1)
                    ev_dx("S", l, lp, 0)
                    ev_dx("V" if i in (4, 5, 6) else "S", l, lp, 1)
                    store_dx(l, 0, lp)
                    store_dx(l, 1, lp)
                if 2 < i < 10:
                    il_t((i - 2) // 2, i % 2)
                if i == 2:
                    il_g(1, 2)
                    il_g(1, 3)
                if i < 9:
                    q_f(m, mp)
                if 3 < i < 11:
                    q_t((i - 3) // 2, (i - 3) % 2)
                if i == 2:
                    q_g(1, 1)
                if i == 3:
                    q_t(0, 0)
                if i in [2,3,5]:
                    il_x([2,3,5].index(i) + 1)
                if i in [3,4,6]:
                    q_x([3,4,6].index(i) + 1)
            mm_o1(3, 0)
            mm_o1(3, 1)
            ev_o1("S", 0)
            ev_o1("V", 1)
